import numpy as np
import ml_dtypes

BF16 = ml_dtypes.bfloat16


def bf(x):
    return np.asarray(x, np.float32).astype(BF16)


def f32(x):
    return np.asarray(x, np.float32)


def f64(x):
    return np.asarray(x).astype(np.float64)


def striped(idx):
    return np.tile(idx.reshape(-1, 16).T, (8, 1))


B, K, Q, S, N = 128, 3, 7, 2048, 2048
EPS = 1e-8


def setup_inputs():
    return {"verts": f32(np.random.standard_normal((K * B, S))), "cams": f32(np.random.standard_normal((B, Q))), "offs": striped(np.random.permutation(np.tile(np.arange(S), 2))[:N])}


def reference(verts, cams, offs):
    idx = offs[:16].T.reshape(-1)
    p = f64(verts).reshape(K, B, S)[:, :, idx]
    cm = f64(cams)
    sc, tx, ty = cm[:, 0:1], cm[:, 1:2], cm[:, 2:3]
    quat = cm[:, 3:]
    quat = quat / (np.sqrt(np.sum(quat * quat, axis=1, keepdims=True)) + EPS)
    qw, qx, qy, qz = quat[:, 0:1], quat[:, 1:2], quat[:, 2:3], quat[:, 3:4]
    r00 = 1.0 - 2.0 * (qy * qy + qz * qz)
    r01 = 2.0 * (qx * qy - qw * qz)
    r02 = 2.0 * (qx * qz + qw * qy)
    r10 = 2.0 * (qx * qy + qw * qz)
    r11 = 1.0 - 2.0 * (qx * qx + qz * qz)
    r12 = 2.0 * (qy * qz - qw * qx)
    u = sc * (r00 * p[0] + r01 * p[1] + r02 * p[2]) + tx
    v = sc * (r10 * p[0] + r11 * p[1] + r12 * p[2]) + ty
    return np.concatenate([u, v], axis=0)

@@ -1,0 +1,106 @@
+import concourse.mybir as mybir
+
+F32 = mybir.dt.float32
+U16 = mybir.dt.uint16
+ALU = mybir.AluOpType
+ACT = mybir.ActivationFunctionType
+
+SAMPLES = 128
+VERTICES = 2048
+PICKS = 2048
+PIECE = 512
+EPS = 1e-8
+QW, QX, QY, QZ = 0, 1, 2, 3
+
+
+def tile_corrlosschamfer_kernel(tc, verts, cams, offs, out):
+    nc = tc.nc
+    with tc.tile_pool(name="held", bufs=1) as held, tc.tile_pool(name="work", bufs=2) as work:
+        offsets = held.tile([128, PICKS // 16], U16, name="offsets")
+        nc.sync.dma_start(offsets[:], offs)
+        cam = held.tile([SAMPLES, 7], F32, name="cam")
+        nc.scalar.dma_start(cam[:], cams)
+        coords = []
+        for k in range(3):
+            coord = held.tile([SAMPLES, VERTICES], F32, name=f"coord{k}")
+            nc.sync.dma_start(coord[:], verts[k * SAMPLES : (k + 1) * SAMPLES, :])
+            coords.append(coord)
+
+        scale = cam[:, 0:1]
+        shift = [cam[:, 1:2], cam[:, 2:3]]
+        quat = cam[:, 3:7]
+
+        squares = held.tile([SAMPLES, 4], F32, name="squares")
+        nc.vector.tensor_tensor(squares[:], quat, quat, ALU.mult)
+        sumsq = held.tile([SAMPLES, 1], F32, name="sumsq")
+        nc.vector.reduce_sum(sumsq[:], squares[:], axis=mybir.AxisListType.X)
+        half = held.tile([SAMPLES, 1], F32, name="half")
+        nc.gpsimd.memset(half[:], 0.5)
+        norm = held.tile([SAMPLES, 1], F32, name="norm")
+        nc.gpsimd.tensor_tensor(norm[:], sumsq[:], half[:], ALU.pow)
+        norm_eps = held.tile([SAMPLES, 1], F32, name="norm_eps")
+        nc.vector.tensor_scalar_add(norm_eps[:], norm[:], EPS)
+        inv_norm = held.tile([SAMPLES, 1], F32, name="inv_norm")
+        nc.vector.reciprocal(inv_norm[:], norm_eps[:])
+        unit = held.tile([SAMPLES, 4], F32, name="unit")
+        nc.vector.tensor_scalar_mul(unit[:], quat, inv_norm[:, 0:1])
+
+        scale2 = held.tile([SAMPLES, 1], F32, name="scale2")
+        nc.vector.tensor_scalar_mul(scale2[:], scale, 2.0)
+        unit_scaled = held.tile([SAMPLES, 4], F32, name="unit_scaled")
+        nc.vector.tensor_scalar_mul(unit_scaled[:], unit[:], scale2[:, 0:1])
+        pair = held.tile([SAMPLES, 16], F32, name="pair")
+        nc.vector.tensor_tensor(
+            pair[:].rearrange("p (i j) -> p i j", i=4),
+            unit_scaled[:].unsqueeze(2).to_broadcast([SAMPLES, 4, 4]),
+            unit[:].unsqueeze(1).to_broadcast([SAMPLES, 4, 4]),
+            ALU.mult,
+        )
+
+        def pr(i, j):
+            return pair[:, 4 * i + j : 4 * i + j + 1]
+
+        coef = held.tile([SAMPLES, 6], F32, name="coef")
+        diag = held.tile([SAMPLES, 2], F32, name="diag")
+        nc.vector.tensor_tensor(diag[:, 0:1], pr(QY, QY), pr(QZ, QZ), ALU.add)
+        nc.vector.tensor_tensor(coef[:, 0:1], scale, diag[:, 0:1], ALU.subtract)
+        nc.vector.tensor_tensor(coef[:, 3:4], pr(QX, QY), pr(QW, QZ), ALU.add)
+        nc.vector.tensor_tensor(coef[:, 1:2], pr(QX, QY), pr(QW, QZ), ALU.subtract)
+        nc.vector.tensor_tensor(diag[:, 1:2], pr(QX, QX), pr(QZ, QZ), ALU.add)
+        nc.vector.tensor_tensor(coef[:, 4:5], scale, diag[:, 1:2], ALU.subtract)
+        nc.vector.tensor_tensor(coef[:, 2:3], pr(QX, QZ), pr(QW, QY), ALU.add)
+        nc.vector.tensor_tensor(coef[:, 5:6], pr(QY, QZ), pr(QW, QX), ALU.subtract)
+
+        spread = {}
+        for k in range(3):
+            for r in range(2):
+                spread[k, r] = held.tile([SAMPLES, PIECE], F32, name=f"spread{k}{r}")
+                nc.scalar.activation(
+                    spread[k, r][:],
+                    coef[:, 3 * r + k : 3 * r + k + 1].to_broadcast([SAMPLES, PIECE]),
+                    ACT.Identity,
+                )
+
+        for piece in range(PICKS // PIECE):
+            first = piece * PIECE
+            piece_offsets = offsets[:, first // 16 : (first + PIECE) // 16]
+            image = [None, None]
+            for k in range(3):
+                for r in range(2):
+                    product = work.tile([SAMPLES, PIECE], F32, name=f"product{k}{r}")
+                    nc.vector.tensor_tensor(
+                        product[:],
+                        coords[k][:].indirect(piece_offsets),
+                        spread[k, r][:],
+                        ALU.mult,
+                    )
+                    total = work.tile([SAMPLES, PIECE], F32, name=f"total{k}{r}")
+                    if k == 0:
+                        nc.scalar.activation(total[:], product[:], ACT.Identity, bias=shift[r])
+                    else:
+                        nc.gpsimd.tensor_tensor(total[:], image[r][:], product[:], ALU.add)
+                    image[r] = total
+            for r in range(2):
+                nc.sync.dma_start(
+                    out[r * SAMPLES : (r + 1) * SAMPLES, first : first + PIECE], image[r][:]
+                )

@@ -1,4 +1,5 @@
 import concourse.mybir as mybir
+from concourse.masks import make_identity
 
 F32 = mybir.dt.float32
 U16 = mybir.dt.uint16
@@ -15,7 +16,11 @@ QW, QX, QY, QZ = 0, 1, 2, 3
 
 def tile_corrlosschamfer_kernel(tc, verts, cams, offs, out):
     nc = tc.nc
-    with tc.tile_pool(name="held", bufs=1) as held, tc.tile_pool(name="work", bufs=2) as work:
+    with (
+        tc.tile_pool(name="held", bufs=1) as held,
+        tc.tile_pool(name="work", bufs=2) as work,
+        tc.psum_pool(name="sums", bufs=2) as sums,
+    ):
         offsets = held.tile([128, PICKS // 16], U16, name="offsets")
         nc.sync.dma_start(offsets[:], offs)
         cam = held.tile([SAMPLES, 7], F32, name="cam")
@@ -81,10 +86,13 @@ def tile_corrlosschamfer_kernel(tc, verts, cams, offs, out):
                     ACT.Identity,
                 )
 
+        identity = held.tile([SAMPLES, SAMPLES], F32, name="identity")
+        make_identity(nc, identity[:])
+
         for piece in range(PICKS // PIECE):
             first = piece * PIECE
             piece_offsets = offsets[:, first // 16 : (first + PIECE) // 16]
-            image = [None, None]
+            total = [sums.tile([SAMPLES, PIECE], F32, name=f"total{r}") for r in range(2)]
             for k in range(3):
                 for r in range(2):
                     product = work.tile([SAMPLES, PIECE], F32, name=f"product{k}{r}")
@@ -94,13 +102,12 @@ def tile_corrlosschamfer_kernel(tc, verts, cams, offs, out):
                         spread[k, r][:],
                         ALU.mult,
                     )
-                    total = work.tile([SAMPLES, PIECE], F32, name=f"total{k}{r}")
-                    if k == 0:
-                        nc.scalar.activation(total[:], product[:], ACT.Identity, bias=shift[r])
-                    else:
-                        nc.gpsimd.tensor_tensor(total[:], image[r][:], product[:], ALU.add)
-                    image[r] = total
+                    nc.tensor.matmul(
+                        total[r][:], identity[:], product[:], start=(k == 0), stop=(k == 2)
+                    )
             for r in range(2):
+                image = work.tile([SAMPLES, PIECE], F32, name=f"image{r}")
+                nc.scalar.activation(image[:], total[r][:], ACT.Identity, bias=shift[r])
                 nc.sync.dma_start(
-                    out[r * SAMPLES : (r + 1) * SAMPLES, first : first + PIECE], image[r][:]
+                    out[r * SAMPLES : (r + 1) * SAMPLES, first : first + PIECE], image[:]
                 )

@@ -31,6 +31,9 @@ def tile_corrlosschamfer_kernel(tc, verts, cams, offs, out):
             nc.sync.dma_start(coord[:], verts[k * SAMPLES : (k + 1) * SAMPLES, :])
             coords.append(coord)
 
+        identity = held.tile([SAMPLES, SAMPLES], F32, name="identity")
+        make_identity(nc, identity[:])
+
         scale = cam[:, 0:1]
         shift = [cam[:, 1:2], cam[:, 2:3]]
         quat = cam[:, 3:7]
@@ -43,38 +46,37 @@ def tile_corrlosschamfer_kernel(tc, verts, cams, offs, out):
         nc.gpsimd.memset(half[:], 0.5)
         norm = held.tile([SAMPLES, 1], F32, name="norm")
         nc.gpsimd.tensor_tensor(norm[:], sumsq[:], half[:], ALU.pow)
-        norm_eps = held.tile([SAMPLES, 1], F32, name="norm_eps")
-        nc.vector.tensor_scalar_add(norm_eps[:], norm[:], EPS)
-        inv_norm = held.tile([SAMPLES, 1], F32, name="inv_norm")
-        nc.vector.reciprocal(inv_norm[:], norm_eps[:])
-        unit = held.tile([SAMPLES, 4], F32, name="unit")
-        nc.vector.tensor_scalar_mul(unit[:], quat, inv_norm[:, 0:1])
 
-        scale2 = held.tile([SAMPLES, 1], F32, name="scale2")
-        nc.vector.tensor_scalar_mul(scale2[:], scale, 2.0)
-        unit_scaled = held.tile([SAMPLES, 4], F32, name="unit_scaled")
-        nc.vector.tensor_scalar_mul(unit_scaled[:], unit[:], scale2[:, 0:1])
         pair = held.tile([SAMPLES, 16], F32, name="pair")
         nc.vector.tensor_tensor(
             pair[:].rearrange("p (i j) -> p i j", i=4),
-            unit_scaled[:].unsqueeze(2).to_broadcast([SAMPLES, 4, 4]),
-            unit[:].unsqueeze(1).to_broadcast([SAMPLES, 4, 4]),
+            quat.unsqueeze(2).to_broadcast([SAMPLES, 4, 4]),
+            quat.unsqueeze(1).to_broadcast([SAMPLES, 4, 4]),
             ALU.mult,
         )
 
         def pr(i, j):
             return pair[:, 4 * i + j : 4 * i + j + 1]
 
-        coef = held.tile([SAMPLES, 6], F32, name="coef")
-        diag = held.tile([SAMPLES, 2], F32, name="diag")
-        nc.vector.tensor_tensor(diag[:, 0:1], pr(QY, QY), pr(QZ, QZ), ALU.add)
-        nc.vector.tensor_tensor(coef[:, 0:1], scale, diag[:, 0:1], ALU.subtract)
-        nc.vector.tensor_tensor(coef[:, 3:4], pr(QX, QY), pr(QW, QZ), ALU.add)
-        nc.vector.tensor_tensor(coef[:, 1:2], pr(QX, QY), pr(QW, QZ), ALU.subtract)
-        nc.vector.tensor_tensor(diag[:, 1:2], pr(QX, QX), pr(QZ, QZ), ALU.add)
-        nc.vector.tensor_tensor(coef[:, 4:5], scale, diag[:, 1:2], ALU.subtract)
-        nc.vector.tensor_tensor(coef[:, 2:3], pr(QX, QZ), pr(QW, QY), ALU.add)
-        nc.vector.tensor_tensor(coef[:, 5:6], pr(QY, QZ), pr(QW, QX), ALU.subtract)
+        mixes = held.tile([SAMPLES, 6], F32, name="mixes")
+        mix = {(k, r): mixes[:, 2 * k + r : 2 * k + r + 1] for k in range(3) for r in range(2)}
+        nc.vector.tensor_scalar(mix[0, 0], pr(QY, QY), pr(QZ, QZ), -1.0, ALU.add, ALU.mult)
+        nc.vector.tensor_tensor(mix[0, 1], pr(QX, QY), pr(QW, QZ), ALU.add)
+        nc.vector.tensor_tensor(mix[1, 0], pr(QX, QY), pr(QW, QZ), ALU.subtract)
+        nc.vector.tensor_scalar(mix[1, 1], pr(QX, QX), pr(QZ, QZ), -1.0, ALU.add, ALU.mult)
+        nc.vector.tensor_tensor(mix[2, 0], pr(QX, QZ), pr(QW, QY), ALU.add)
+        nc.vector.tensor_tensor(mix[2, 1], pr(QY, QZ), pr(QW, QX), ALU.subtract)
+        scale2 = held.tile([SAMPLES, 1], F32, name="scale2")
+        nc.vector.tensor_scalar_mul(scale2[:], scale, 2.0)
+
+        norm_eps = held.tile([SAMPLES, 1], F32, name="norm_eps")
+        nc.vector.tensor_scalar_add(norm_eps[:], norm[:], EPS)
+        inv_norm = held.tile([SAMPLES, 1], F32, name="inv_norm")
+        nc.vector.reciprocal(inv_norm[:], norm_eps[:])
+        gain = held.tile([SAMPLES, 1], F32, name="gain")
+        nc.vector.tensor_scalar(
+            gain[:], inv_norm[:], inv_norm[:, 0:1], scale2[:, 0:1], ALU.mult, ALU.mult
+        )
 
         spread = {}
         for k in range(3):
@@ -82,12 +84,11 @@ def tile_corrlosschamfer_kernel(tc, verts, cams, offs, out):
                 spread[k, r] = held.tile([SAMPLES, PIECE], F32, name=f"spread{k}{r}")
                 nc.scalar.activation(
                     spread[k, r][:],
-                    coef[:, 3 * r + k : 3 * r + k + 1].to_broadcast([SAMPLES, PIECE]),
+                    mix[k, r].to_broadcast([SAMPLES, PIECE]),
                     ACT.Identity,
+                    bias=(scale if r == k else 0.0),
+                    scale=gain[:, 0:1],
                 )
-
-        identity = held.tile([SAMPLES, SAMPLES], F32, name="identity")
-        make_identity(nc, identity[:])
 
         for piece in range(PICKS // PIECE):
             first = piece * PIECE

@@ -9,7 +9,9 @@ ACT = mybir.ActivationFunctionType
 SAMPLES = 128
 VERTICES = 2048
 PICKS = 2048
-PIECE = 512
+PIECES = (512, 512, 512, 384, 128)
+WIDEST = max(PIECES)
+assert sum(PIECES) == PICKS and all(width % 32 == 0 for width in PIECES)
 EPS = 1e-8
 QW, QX, QY, QZ = 0, 1, 2, 3
 
@@ -81,34 +83,35 @@ def tile_corrlosschamfer_kernel(tc, verts, cams, offs, out):
         spread = {}
         for k in range(3):
             for r in range(2):
-                spread[k, r] = held.tile([SAMPLES, PIECE], F32, name=f"spread{k}{r}")
+                spread[k, r] = held.tile([SAMPLES, WIDEST], F32, name=f"spread{k}{r}")
                 nc.scalar.activation(
                     spread[k, r][:],
-                    mix[k, r].to_broadcast([SAMPLES, PIECE]),
+                    mix[k, r].to_broadcast([SAMPLES, WIDEST]),
                     ACT.Identity,
                     bias=(scale if r == k else 0.0),
                     scale=gain[:, 0:1],
                 )
 
-        for piece in range(PICKS // PIECE):
-            first = piece * PIECE
-            piece_offsets = offsets[:, first // 16 : (first + PIECE) // 16]
-            total = [sums.tile([SAMPLES, PIECE], F32, name=f"total{r}") for r in range(2)]
+        first = 0
+        for width in PIECES:
+            piece_offsets = offsets[:, first // 16 : (first + width) // 16]
+            total = [sums.tile([SAMPLES, width], F32, name=f"total{r}") for r in range(2)]
             for k in range(3):
                 for r in range(2):
-                    product = work.tile([SAMPLES, PIECE], F32, name=f"product{k}{r}")
+                    product = work.tile([SAMPLES, width], F32, name=f"product{k}{r}")
                     nc.vector.tensor_tensor(
                         product[:],
                         coords[k][:].indirect(piece_offsets),
-                        spread[k, r][:],
+                        spread[k, r][:, 0:width],
                         ALU.mult,
                     )
                     nc.tensor.matmul(
                         total[r][:], identity[:], product[:], start=(k == 0), stop=(k == 2)
                     )
             for r in range(2):
-                image = work.tile([SAMPLES, PIECE], F32, name=f"image{r}")
+                image = work.tile([SAMPLES, width], F32, name=f"image{r}")
                 nc.scalar.activation(image[:], total[r][:], ACT.Identity, bias=shift[r])
                 nc.sync.dma_start(
-                    out[r * SAMPLES : (r + 1) * SAMPLES, first : first + PIECE], image[:]
+                    out[r * SAMPLES : (r + 1) * SAMPLES, first : first + width], image[:]
                 )
+            first += width

@@ -12,6 +12,7 @@ PICKS = 2048
 PIECES = (512, 512, 512, 384, 128)
 WIDEST = max(PIECES)
 assert sum(PIECES) == PICKS and all(width % 32 == 0 for width in PIECES)
+WARMUPS = 10
 EPS = 1e-8
 QW, QX, QY, QZ = 0, 1, 2, 3
 
@@ -35,6 +36,9 @@ def tile_corrlosschamfer_kernel(tc, verts, cams, offs, out):
 
         identity = held.tile([SAMPLES, SAMPLES], F32, name="identity")
         make_identity(nc, identity[:])
+        warmup = sums.tile([SAMPLES, SAMPLES], F32, name="warmup")
+        for turn in range(WARMUPS):
+            nc.tensor.matmul(warmup[:], identity[:], identity[:], start=True, stop=True)
 
         scale = cam[:, 0:1]
         shift = [cam[:, 1:2], cam[:, 2:3]]

@@ -14,6 +14,7 @@ WIDEST = max(PIECES)
 assert sum(PIECES) == PICKS and all(width % 32 == 0 for width in PIECES)
 WARMUPS = 10
 EPS = 1e-8
+TINY = 1e-30
 QW, QX, QY, QZ = 0, 1, 2, 3
 
 
@@ -21,7 +22,7 @@ def tile_corrlosschamfer_kernel(tc, verts, cams, offs, out):
     nc = tc.nc
     with (
         tc.tile_pool(name="held", bufs=1) as held,
-        tc.tile_pool(name="work", bufs=2) as work,
+        tc.tile_pool(name="work", bufs=len(PIECES)) as work,
         tc.psum_pool(name="sums", bufs=2) as sums,
     ):
         offsets = held.tile([128, PICKS // 16], U16, name="offsets")
@@ -65,57 +66,96 @@ def tile_corrlosschamfer_kernel(tc, verts, cams, offs, out):
             return pair[:, 4 * i + j : 4 * i + j + 1]
 
         mixes = held.tile([SAMPLES, 6], F32, name="mixes")
-        mix = {(k, r): mixes[:, 2 * k + r : 2 * k + r + 1] for k in range(3) for r in range(2)}
+        mix = {(r, k): mixes[:, 3 * r + k : 3 * r + k + 1] for r in range(2) for k in range(3)}
         nc.vector.tensor_scalar(mix[0, 0], pr(QY, QY), pr(QZ, QZ), -1.0, ALU.add, ALU.mult)
-        nc.vector.tensor_tensor(mix[0, 1], pr(QX, QY), pr(QW, QZ), ALU.add)
-        nc.vector.tensor_tensor(mix[1, 0], pr(QX, QY), pr(QW, QZ), ALU.subtract)
+        nc.vector.tensor_tensor(mix[0, 1], pr(QX, QY), pr(QW, QZ), ALU.subtract)
+        nc.vector.tensor_tensor(mix[0, 2], pr(QX, QZ), pr(QW, QY), ALU.add)
+        nc.vector.tensor_tensor(mix[1, 0], pr(QX, QY), pr(QW, QZ), ALU.add)
         nc.vector.tensor_scalar(mix[1, 1], pr(QX, QX), pr(QZ, QZ), -1.0, ALU.add, ALU.mult)
-        nc.vector.tensor_tensor(mix[2, 0], pr(QX, QZ), pr(QW, QY), ALU.add)
-        nc.vector.tensor_tensor(mix[2, 1], pr(QY, QZ), pr(QW, QX), ALU.subtract)
-        scale2 = held.tile([SAMPLES, 1], F32, name="scale2")
-        nc.vector.tensor_scalar_mul(scale2[:], scale, 2.0)
+        nc.vector.tensor_tensor(mix[1, 2], pr(QY, QZ), pr(QW, QX), ALU.subtract)
+        diagonal = held.tile([SAMPLES, 6], F32, name="diagonal")
+        nc.gpsimd.memset(diagonal[:], 0.0)
+        nc.gpsimd.memset(diagonal[:, 0:1], 1.0)
+        nc.gpsimd.memset(diagonal[:, 4:5], 1.0)
 
         norm_eps = held.tile([SAMPLES, 1], F32, name="norm_eps")
         nc.vector.tensor_scalar_add(norm_eps[:], norm[:], EPS)
         inv_norm = held.tile([SAMPLES, 1], F32, name="inv_norm")
         nc.vector.reciprocal(inv_norm[:], norm_eps[:])
         gain = held.tile([SAMPLES, 1], F32, name="gain")
-        nc.vector.tensor_scalar(
-            gain[:], inv_norm[:], inv_norm[:, 0:1], scale2[:, 0:1], ALU.mult, ALU.mult
+        nc.vector.tensor_scalar(gain[:], inv_norm[:], inv_norm[:, 0:1], 2.0, ALU.mult, ALU.mult)
+        rot = held.tile([SAMPLES, 6], F32, name="rot")
+        nc.vector.scalar_tensor_tensor(
+            rot[:], mixes[:], gain[:, 0:1], diagonal[:], ALU.mult, ALU.add
         )
 
-        spread = {}
+        rot_sq = held.tile([SAMPLES, 6], F32, name="rot_sq")
+        nc.vector.tensor_tensor(rot_sq[:], rot[:], rot[:], ALU.mult)
+        row0_wins = held.tile([SAMPLES, 3], F32, name="row0_wins")
+        nc.vector.tensor_tensor(row0_wins[:], rot_sq[:, 0:3], rot_sq[:, 3:6], ALU.is_ge)
+        step = held.tile([SAMPLES, 3], F32, name="step")
+        nc.vector.tensor_tensor(step[:], rot[:, 0:3], rot[:, 3:6], ALU.subtract)
+        taken = held.tile([SAMPLES, 3], F32, name="taken")
+        nc.vector.tensor_tensor(taken[:], step[:], row0_wins[:], ALU.mult)
+        pivot = held.tile([SAMPLES, 3], F32, name="pivot")
+        nc.vector.tensor_tensor(pivot[:], rot[:, 3:6], taken[:], ALU.add)
+
+        spread = []
         for k in range(3):
-            for r in range(2):
-                spread[k, r] = held.tile([SAMPLES, WIDEST], F32, name=f"spread{k}{r}")
-                nc.scalar.activation(
-                    spread[k, r][:],
-                    mix[k, r].to_broadcast([SAMPLES, WIDEST]),
-                    ACT.Identity,
-                    bias=(scale if r == k else 0.0),
-                    scale=gain[:, 0:1],
-                )
+            spread.append(held.tile([SAMPLES, WIDEST], F32, name=f"spread{k}"))
+            nc.scalar.activation(
+                spread[k][:], pivot[:, k : k + 1].to_broadcast([SAMPLES, WIDEST]), ACT.Identity
+            )
+
+        pivot_sq = held.tile([SAMPLES, 3], F32, name="pivot_sq")
+        nc.vector.tensor_tensor(pivot_sq[:], rot_sq[:, 0:3], rot_sq[:, 3:6], ALU.max)
+        divisor = held.tile([SAMPLES, 3], F32, name="divisor")
+        nc.vector.tensor_scalar_add(divisor[:], pivot_sq[:], TINY)
+        inv_divisor = held.tile([SAMPLES, 3], F32, name="inv_divisor")
+        nc.vector.reciprocal(inv_divisor[:], divisor[:])
+        weight = held.tile([SAMPLES, 3], F32, name="weight")
+        nc.vector.scalar_tensor_tensor(
+            weight[:], pivot[:], scale, inv_divisor[:], ALU.mult, ALU.mult
+        )
+        factors = held.tile([SAMPLES, 6], F32, name="factors")
+        nc.vector.tensor_tensor(
+            factors[:].rearrange("p (r k) -> p r k", r=2),
+            rot[:].rearrange("p (r k) -> p r k", r=2),
+            weight[:].unsqueeze(1).to_broadcast([SAMPLES, 2, 3]),
+            ALU.mult,
+        )
+        factor = {(r, k): factors[:, 3 * r + k : 3 * r + k + 1] for r in range(2) for k in range(3)}
+
+        weights0 = []
+        for k in range(3):
+            weights0.append(held.tile([SAMPLES, SAMPLES], F32, name=f"weights0{k}"))
+            nc.scalar.activation(weights0[k][:], identity[:], ACT.Identity, scale=factor[0, k])
 
         first = 0
         for width in PIECES:
             piece_offsets = offsets[:, first // 16 : (first + width) // 16]
-            total = [sums.tile([SAMPLES, width], F32, name=f"total{r}") for r in range(2)]
+            total0 = sums.tile([SAMPLES, width], F32, name="total0")
+            total1 = None
             for k in range(3):
-                for r in range(2):
-                    product = work.tile([SAMPLES, width], F32, name=f"product{k}{r}")
-                    nc.vector.tensor_tensor(
-                        product[:],
-                        coords[k][:].indirect(piece_offsets),
-                        spread[k, r][:, 0:width],
-                        ALU.mult,
-                    )
-                    nc.tensor.matmul(
-                        total[r][:], identity[:], product[:], start=(k == 0), stop=(k == 2)
-                    )
-            for r in range(2):
-                image = work.tile([SAMPLES, width], F32, name=f"image{r}")
-                nc.scalar.activation(image[:], total[r][:], ACT.Identity, bias=shift[r])
-                nc.sync.dma_start(
-                    out[r * SAMPLES : (r + 1) * SAMPLES, first : first + width], image[:]
+                picked = work.tile([SAMPLES, width], F32, name=f"picked{k}")
+                nc.vector.tensor_tensor(
+                    picked[:], coords[k][:].indirect(piece_offsets), spread[k][:, 0:width], ALU.mult
                 )
+                nc.tensor.matmul(
+                    total0[:], weights0[k][:], picked[:], start=(k == 0), stop=(k == 2)
+                )
+                longer = work.tile([SAMPLES, width], F32, name=f"total1{k}")
+                if k == 0:
+                    nc.scalar.activation(
+                        longer[:], picked[:], ACT.Identity, bias=shift[1], scale=factor[1, 0]
+                    )
+                else:
+                    nc.vector.scalar_tensor_tensor(
+                        longer[:], picked[:], factor[1, k], total1[:], ALU.mult, ALU.add
+                    )
+                total1 = longer
+            image0 = work.tile([SAMPLES, width], F32, name="image0")
+            nc.scalar.activation(image0[:], total0[:], ACT.Identity, bias=shift[0])
+            nc.sync.dma_start(out[0:SAMPLES, first : first + width], image0[:])
+            nc.sync.dma_start(out[SAMPLES : 2 * SAMPLES, first : first + width], total1[:])
             first += width

@@ -9,22 +9,25 @@ ACT = mybir.ActivationFunctionType
 SAMPLES = 128
 VERTICES = 2048
 PICKS = 2048
+BANK = 512
+BLOCK = 1024
+FIRST_CUTS = (512, 512)
+LAST_CUTS = (512, 384, 128)
 PIECES = (512, 512, 512, 384, 128)
-WIDEST = max(PIECES)
-assert sum(PIECES) == PICKS and all(width % 32 == 0 for width in PIECES)
 WARMUPS = 10
 EPS = 1e-8
 TINY = 1e-30
 QW, QX, QY, QZ = 0, 1, 2, 3
 
 
+def spans(first, widths):
+    assert all(width % 32 == 0 for width in widths)
+    return [(first + sum(widths[:i]), width) for i, width in enumerate(widths)]
+
+
 def tile_corrlosschamfer_kernel(tc, verts, cams, offs, out):
     nc = tc.nc
-    with (
-        tc.tile_pool(name="held", bufs=1) as held,
-        tc.tile_pool(name="work", bufs=len(PIECES)) as work,
-        tc.psum_pool(name="sums", bufs=2) as sums,
-    ):
+    with tc.tile_pool(name="held", bufs=1) as held, tc.psum_pool(name="sums", bufs=1) as sums:
         offsets = held.tile([128, PICKS // 16], U16, name="offsets")
         nc.sync.dma_start(offsets[:], offs)
         cam = held.tile([SAMPLES, 7], F32, name="cam")
@@ -91,26 +94,33 @@ def tile_corrlosschamfer_kernel(tc, verts, cams, offs, out):
 
         rot_sq = held.tile([SAMPLES, 6], F32, name="rot_sq")
         nc.vector.tensor_tensor(rot_sq[:], rot[:], rot[:], ALU.mult)
-        row0_wins = held.tile([SAMPLES, 3], F32, name="row0_wins")
-        nc.vector.tensor_tensor(row0_wins[:], rot_sq[:, 0:3], rot_sq[:, 3:6], ALU.is_ge)
         step = held.tile([SAMPLES, 3], F32, name="step")
         nc.vector.tensor_tensor(step[:], rot[:, 0:3], rot[:, 3:6], ALU.subtract)
-        taken = held.tile([SAMPLES, 3], F32, name="taken")
-        nc.vector.tensor_tensor(taken[:], step[:], row0_wins[:], ALU.mult)
-        pivot = held.tile([SAMPLES, 3], F32, name="pivot")
-        nc.vector.tensor_tensor(pivot[:], rot[:, 3:6], taken[:], ALU.add)
-
-        spread = []
-        for k in range(3):
-            spread.append(held.tile([SAMPLES, WIDEST], F32, name=f"spread{k}"))
-            nc.scalar.activation(
-                spread[k][:], pivot[:, k : k + 1].to_broadcast([SAMPLES, WIDEST]), ACT.Identity
-            )
-
+        row0_wins = held.tile([SAMPLES, 3], F32, name="row0_wins")
+        nc.vector.tensor_tensor(row0_wins[:], rot_sq[:, 0:3], rot_sq[:, 3:6], ALU.is_ge)
         pivot_sq = held.tile([SAMPLES, 3], F32, name="pivot_sq")
         nc.vector.tensor_tensor(pivot_sq[:], rot_sq[:, 0:3], rot_sq[:, 3:6], ALU.max)
+
+        spread = [held.tile([SAMPLES, BLOCK], F32, name=f"spread{k}") for k in range(3)]
+
+        def spread_pivot(k):
+            for start in range(0, BLOCK, BANK):
+                nc.scalar.activation(
+                    spread[k][:, start : start + BANK],
+                    step[:, k : k + 1].to_broadcast([SAMPLES, BANK]),
+                    ACT.Identity,
+                    bias=rot[:, 3 + k : 4 + k],
+                    scale=row0_wins[:, k : k + 1],
+                )
+
+        spread_pivot(0)
+
+        taken = held.tile([SAMPLES, 3], F32, name="taken")
+        nc.vector.tensor_tensor(taken[:], step[:], row0_wins[:], ALU.mult)
         divisor = held.tile([SAMPLES, 3], F32, name="divisor")
         nc.vector.tensor_scalar_add(divisor[:], pivot_sq[:], TINY)
+        pivot = held.tile([SAMPLES, 3], F32, name="pivot")
+        nc.vector.tensor_tensor(pivot[:], rot[:, 3:6], taken[:], ALU.add)
         inv_divisor = held.tile([SAMPLES, 3], F32, name="inv_divisor")
         nc.vector.reciprocal(inv_divisor[:], divisor[:])
         weight = held.tile([SAMPLES, 3], F32, name="weight")
@@ -126,36 +136,66 @@ def tile_corrlosschamfer_kernel(tc, verts, cams, offs, out):
         )
         factor = {(r, k): factors[:, 3 * r + k : 3 * r + k + 1] for r in range(2) for k in range(3)}
 
-        weights0 = []
-        for k in range(3):
-            weights0.append(held.tile([SAMPLES, SAMPLES], F32, name=f"weights0{k}"))
-            nc.scalar.activation(weights0[k][:], identity[:], ACT.Identity, scale=factor[0, k])
-
-        first = 0
-        for width in PIECES:
-            piece_offsets = offsets[:, first // 16 : (first + width) // 16]
-            total0 = sums.tile([SAMPLES, width], F32, name="total0")
-            total1 = None
+        picked = [held.tile([SAMPLES, PICKS], F32, name=f"picked{k}") for k in range(3)]
+        weights0 = [held.tile([SAMPLES, SAMPLES], F32, name=f"weights0{k}") for k in range(3)]
+        total0 = [sums.tile([SAMPLES, cols], F32, name=f"total0{p}") for p, cols in enumerate(PIECES)]
+        total1 = [held.tile([SAMPLES, PICKS], F32, name=f"total1{k}") for k in range(3)]
+        image0 = held.tile([SAMPLES, PICKS], F32, name="image0")
+        blocks = PICKS // BLOCK
+        for block in range(blocks):
             for k in range(3):
-                picked = work.tile([SAMPLES, width], F32, name=f"picked{k}")
-                nc.vector.tensor_tensor(
-                    picked[:], coords[k][:].indirect(piece_offsets), spread[k][:, 0:width], ALU.mult
-                )
-                nc.tensor.matmul(
-                    total0[:], weights0[k][:], picked[:], start=(k == 0), stop=(k == 2)
-                )
-                longer = work.tile([SAMPLES, width], F32, name=f"total1{k}")
-                if k == 0:
+                if block == 0:
                     nc.scalar.activation(
-                        longer[:], picked[:], ACT.Identity, bias=shift[1], scale=factor[1, 0]
+                        weights0[k][:], identity[:], ACT.Identity, scale=factor[0, k]
                     )
-                else:
-                    nc.vector.scalar_tensor_tensor(
-                        longer[:], picked[:], factor[1, k], total1[:], ALU.mult, ALU.add
+                    if k < 2:
+                        spread_pivot(k + 1)
+                widths = (BLOCK,)
+                if (block, k) == (0, 0):
+                    widths = FIRST_CUTS
+                if (block, k) == (blocks - 1, 2):
+                    widths = LAST_CUTS
+                assert sum(widths) == BLOCK
+                for first, width in spans(block * BLOCK, widths):
+                    cut = slice(first, first + width)
+                    nc.vector.tensor_tensor(
+                        picked[k][:, cut],
+                        coords[k][:].indirect(offsets[:, first // 16 : (first + width) // 16]),
+                        spread[k][:, 0:width],
+                        ALU.mult,
                     )
-                total1 = longer
-            image0 = work.tile([SAMPLES, width], F32, name="image0")
-            nc.scalar.activation(image0[:], total0[:], ACT.Identity, bias=shift[0])
-            nc.sync.dma_start(out[0:SAMPLES, first : first + width], image0[:])
-            nc.sync.dma_start(out[SAMPLES : 2 * SAMPLES, first : first + width], total1[:])
-            first += width
+                    if k == 0:
+                        nc.scalar.activation(
+                            total1[0][:, cut],
+                            picked[0][:, cut],
+                            ACT.Identity,
+                            bias=shift[1],
+                            scale=factor[1, 0],
+                        )
+                    else:
+                        nc.vector.scalar_tensor_tensor(
+                            total1[k][:, cut],
+                            picked[k][:, cut],
+                            factor[1, k],
+                            total1[k - 1][:, cut],
+                            ALU.mult,
+                            ALU.add,
+                        )
+                    if k == 2:
+                        nc.sync.dma_start(out[SAMPLES : 2 * SAMPLES, cut], total1[2][:, cut])
+                    for p, (start, cols) in enumerate(spans(0, PIECES)):
+                        if first <= start < first + width:
+                            piece = slice(start, start + cols)
+                            nc.tensor.matmul(
+                                total0[p][:],
+                                weights0[k][:],
+                                picked[k][:, piece],
+                                start=(k == 0),
+                                stop=(k == 2),
+                            )
+                            if k == 2:
+                                nc.scalar.activation(
+                                    image0[:, piece], total0[p][:], ACT.Identity, bias=shift[0]
+                                )
+                    if k == 2:
+                        nc.sync.dma_start(out[0:SAMPLES, cut], image0[:, cut])

@@ -9,25 +9,21 @@ ACT = mybir.ActivationFunctionType
 SAMPLES = 128
 VERTICES = 2048
 PICKS = 2048
-BANK = 512
-BLOCK = 1024
-FIRST_CUTS = (512, 512)
-LAST_CUTS = (512, 384, 128)
 PIECES = (512, 512, 512, 384, 128)
-WARMUPS = 10
+WIDEST = max(PIECES)
+assert sum(PIECES) == PICKS and all(width % 32 == 0 for width in PIECES)
 EPS = 1e-8
 TINY = 1e-30
 QW, QX, QY, QZ = 0, 1, 2, 3
 
 
-def spans(first, widths):
-    assert all(width % 32 == 0 for width in widths)
-    return [(first + sum(widths[:i]), width) for i, width in enumerate(widths)]
-
-
 def tile_corrlosschamfer_kernel(tc, verts, cams, offs, out):
     nc = tc.nc
-    with tc.tile_pool(name="held", bufs=1) as held, tc.psum_pool(name="sums", bufs=1) as sums:
+    with (
+        tc.tile_pool(name="held", bufs=1) as held,
+        tc.tile_pool(name="work", bufs=len(PIECES)) as work,
+        tc.psum_pool(name="sums", bufs=2) as sums,
+    ):
         offsets = held.tile([128, PICKS // 16], U16, name="offsets")
         nc.sync.dma_start(offsets[:], offs)
         cam = held.tile([SAMPLES, 7], F32, name="cam")
@@ -37,23 +33,23 @@ def tile_corrlosschamfer_kernel(tc, verts, cams, offs, out):
             coord = held.tile([SAMPLES, VERTICES], F32, name=f"coord{k}")
             nc.sync.dma_start(coord[:], verts[k * SAMPLES : (k + 1) * SAMPLES, :])
             coords.append(coord)
-
-        identity = held.tile([SAMPLES, SAMPLES], F32, name="identity")
-        make_identity(nc, identity[:])
-        warmup = sums.tile([SAMPLES, SAMPLES], F32, name="warmup")
-        for turn in range(WARMUPS):
-            nc.tensor.matmul(warmup[:], identity[:], identity[:], start=True, stop=True)
-
         scale = cam[:, 0:1]
         shift = [cam[:, 1:2], cam[:, 2:3]]
         quat = cam[:, 3:7]
+
+        identity = held.tile([SAMPLES, SAMPLES], F32, name="identity")
+        make_identity(nc, identity[:])
+        half = held.tile([SAMPLES, 1], F32, name="half")
+        nc.gpsimd.memset(half[:], 0.5)
+        diagonal = held.tile([SAMPLES, 6], F32, name="diagonal")
+        nc.gpsimd.memset(diagonal[:], 0.0)
+        nc.gpsimd.memset(diagonal[:, 0:1], 1.0)
+        nc.gpsimd.memset(diagonal[:, 4:5], 1.0)
 
         squares = held.tile([SAMPLES, 4], F32, name="squares")
         nc.vector.tensor_tensor(squares[:], quat, quat, ALU.mult)
         sumsq = held.tile([SAMPLES, 1], F32, name="sumsq")
         nc.vector.reduce_sum(sumsq[:], squares[:], axis=mybir.AxisListType.X)
-        half = held.tile([SAMPLES, 1], F32, name="half")
-        nc.gpsimd.memset(half[:], 0.5)
         norm = held.tile([SAMPLES, 1], F32, name="norm")
         nc.gpsimd.tensor_tensor(norm[:], sumsq[:], half[:], ALU.pow)
 
@@ -76,10 +72,6 @@ def tile_corrlosschamfer_kernel(tc, verts, cams, offs, out):
         nc.vector.tensor_tensor(mix[1, 0], pr(QX, QY), pr(QW, QZ), ALU.add)
         nc.vector.tensor_scalar(mix[1, 1], pr(QX, QX), pr(QZ, QZ), -1.0, ALU.add, ALU.mult)
         nc.vector.tensor_tensor(mix[1, 2], pr(QY, QZ), pr(QW, QX), ALU.subtract)
-        diagonal = held.tile([SAMPLES, 6], F32, name="diagonal")
-        nc.gpsimd.memset(diagonal[:], 0.0)
-        nc.gpsimd.memset(diagonal[:, 0:1], 1.0)
-        nc.gpsimd.memset(diagonal[:, 4:5], 1.0)
 
         norm_eps = held.tile([SAMPLES, 1], F32, name="norm_eps")
         nc.vector.tensor_scalar_add(norm_eps[:], norm[:], EPS)
@@ -91,36 +83,34 @@ def tile_corrlosschamfer_kernel(tc, verts, cams, offs, out):
         nc.vector.scalar_tensor_tensor(
             rot[:], mixes[:], gain[:, 0:1], diagonal[:], ALU.mult, ALU.add
         )
+        row0, row1 = rot[:, 0:3], rot[:, 3:6]
 
         rot_sq = held.tile([SAMPLES, 6], F32, name="rot_sq")
         nc.vector.tensor_tensor(rot_sq[:], rot[:], rot[:], ALU.mult)
         step = held.tile([SAMPLES, 3], F32, name="step")
-        nc.vector.tensor_tensor(step[:], rot[:, 0:3], rot[:, 3:6], ALU.subtract)
+        nc.vector.tensor_tensor(step[:], row0, row1, ALU.subtract)
         row0_wins = held.tile([SAMPLES, 3], F32, name="row0_wins")
         nc.vector.tensor_tensor(row0_wins[:], rot_sq[:, 0:3], rot_sq[:, 3:6], ALU.is_ge)
+
+        spread = []
+        for k in range(3):
+            spread.append(held.tile([SAMPLES, WIDEST], F32, name=f"spread{k}"))
+            nc.scalar.activation(
+                spread[k][:],
+                step[:, k : k + 1].to_broadcast([SAMPLES, WIDEST]),
+                ACT.Identity,
+                bias=rot[:, 3 + k : 4 + k],
+                scale=row0_wins[:, k : k + 1],
+            )
+
         pivot_sq = held.tile([SAMPLES, 3], F32, name="pivot_sq")
         nc.vector.tensor_tensor(pivot_sq[:], rot_sq[:, 0:3], rot_sq[:, 3:6], ALU.max)
-
-        spread = [held.tile([SAMPLES, BLOCK], F32, name=f"spread{k}") for k in range(3)]
-
-        def spread_pivot(k):
-            for start in range(0, BLOCK, BANK):
-                nc.scalar.activation(
-                    spread[k][:, start : start + BANK],
-                    step[:, k : k + 1].to_broadcast([SAMPLES, BANK]),
-                    ACT.Identity,
-                    bias=rot[:, 3 + k : 4 + k],
-                    scale=row0_wins[:, k : k + 1],
-                )
-
-        spread_pivot(0)
-
         taken = held.tile([SAMPLES, 3], F32, name="taken")
         nc.vector.tensor_tensor(taken[:], step[:], row0_wins[:], ALU.mult)
         divisor = held.tile([SAMPLES, 3], F32, name="divisor")
         nc.vector.tensor_scalar_add(divisor[:], pivot_sq[:], TINY)
         pivot = held.tile([SAMPLES, 3], F32, name="pivot")
-        nc.vector.tensor_tensor(pivot[:], rot[:, 3:6], taken[:], ALU.add)
+        nc.vector.tensor_tensor(pivot[:], row1, taken[:], ALU.add)
         inv_divisor = held.tile([SAMPLES, 3], F32, name="inv_divisor")
         nc.vector.reciprocal(inv_divisor[:], divisor[:])
         weight = held.tile([SAMPLES, 3], F32, name="weight")
@@ -136,66 +126,36 @@ def tile_corrlosschamfer_kernel(tc, verts, cams, offs, out):
         )
         factor = {(r, k): factors[:, 3 * r + k : 3 * r + k + 1] for r in range(2) for k in range(3)}
 
-        picked = [held.tile([SAMPLES, PICKS], F32, name=f"picked{k}") for k in range(3)]
-        weights0 = [held.tile([SAMPLES, SAMPLES], F32, name=f"weights0{k}") for k in range(3)]
-        total0 = [sums.tile([SAMPLES, cols], F32, name=f"total0{p}") for p, cols in enumerate(PIECES)]
-        total1 = [held.tile([SAMPLES, PICKS], F32, name=f"total1{k}") for k in range(3)]
-        image0 = held.tile([SAMPLES, PICKS], F32, name="image0")
-        blocks = PICKS // BLOCK
-        for block in range(blocks):
+        weights0 = []
+        for k in range(3):
+            weights0.append(held.tile([SAMPLES, SAMPLES], F32, name=f"weights0{k}"))
+            nc.scalar.activation(weights0[k][:], identity[:], ACT.Identity, scale=factor[0, k])
+
+        first = 0
+        for width in PIECES:
+            piece_offsets = offsets[:, first // 16 : (first + width) // 16]
+            total0 = sums.tile([SAMPLES, width], F32, name="total0")
+            total1 = None
             for k in range(3):
-                if block == 0:
+                picked = work.tile([SAMPLES, width], F32, name=f"picked{k}")
+                nc.vector.tensor_tensor(
+                    picked[:], coords[k][:].indirect(piece_offsets), spread[k][:, 0:width], ALU.mult
+                )
+                nc.tensor.matmul(
+                    total0[:], weights0[k][:], picked[:], start=(k == 0), stop=(k == 2)
+                )
+                summed = work.tile([SAMPLES, width], F32, name=f"total1{k}")
+                if k == 0:
                     nc.scalar.activation(
-                        weights0[k][:], identity[:], ACT.Identity, scale=factor[0, k]
+                        summed[:], picked[:], ACT.Identity, bias=shift[1], scale=factor[1, 0]
                     )
-                    if k < 2:
-                        spread_pivot(k + 1)
-                widths = (BLOCK,)
-                if (block, k) == (0, 0):
-                    widths = FIRST_CUTS
-                if (block, k) == (blocks - 1, 2):
-                    widths = LAST_CUTS
-                assert sum(widths) == BLOCK
-                for first, width in spans(block * BLOCK, widths):
-                    cut = slice(first, first + width)
-                    nc.vector.tensor_tensor(
-                        picked[k][:, cut],
-                        coords[k][:].indirect(offsets[:, first // 16 : (first + width) // 16]),
-                        spread[k][:, 0:width],
-                        ALU.mult,
+                else:
+                    nc.vector.scalar_tensor_tensor(
+                        summed[:], picked[:], factor[1, k], total1[:], ALU.mult, ALU.add
                     )
-                    if k == 0:
-                        nc.scalar.activation(
-                            total1[0][:, cut],
-                            picked[0][:, cut],
-                            ACT.Identity,
-                            bias=shift[1],
-                            scale=factor[1, 0],
-                        )
-                    else:
-                        nc.vector.scalar_tensor_tensor(
-                            total1[k][:, cut],
-                            picked[k][:, cut],
-                            factor[1, k],
-                            total1[k - 1][:, cut],
-                            ALU.mult,
-                            ALU.add,
-                        )
-                    if k == 2:
-                        nc.sync.dma_start(out[SAMPLES : 2 * SAMPLES, cut], total1[2][:, cut])
-                    for p, (start, cols) in enumerate(spans(0, PIECES)):
-                        if first <= start < first + width:
-                            piece = slice(start, start + cols)
-                            nc.tensor.matmul(
-                                total0[p][:],
-                                weights0[k][:],
-                                picked[k][:, piece],
-                                start=(k == 0),
-                                stop=(k == 2),
-                            )
-                            if k == 2:
-                                nc.scalar.activation(
-                                    image0[:, piece], total0[p][:], ACT.Identity, bias=shift[0]
-                                )
-                    if k == 2:
-                        nc.sync.dma_start(out[0:SAMPLES, cut], image0[:, cut])
+                total1 = summed
+            nc.sync.dma_start(out[SAMPLES : 2 * SAMPLES, first : first + width], total1[:])
+            image0 = work.tile([SAMPLES, width], F32, name="image0")
+            nc.scalar.activation(image0[:], total0[:], ACT.Identity, bias=shift[0])
+            nc.sync.dma_start(out[0:SAMPLES, first : first + width], image0[:])
+            first += width

@@ -44,14 +44,9 @@ def tile_corrlosschamfer_kernel(tc, verts, cams, offs, out):
         diagonal = held.tile([SAMPLES, 6], F32, name="diagonal")
         nc.gpsimd.memset(diagonal[:], 0.0)
         nc.gpsimd.memset(diagonal[:, 0:1], 1.0)
-        nc.gpsimd.memset(diagonal[:, 4:5], 1.0)
-
-        squares = held.tile([SAMPLES, 4], F32, name="squares")
-        nc.vector.tensor_tensor(squares[:], quat, quat, ALU.mult)
-        sumsq = held.tile([SAMPLES, 1], F32, name="sumsq")
-        nc.vector.reduce_sum(sumsq[:], squares[:], axis=mybir.AxisListType.X)
-        norm = held.tile([SAMPLES, 1], F32, name="norm")
-        nc.gpsimd.tensor_tensor(norm[:], sumsq[:], half[:], ALU.pow)
+        nc.gpsimd.memset(diagonal[:, 3:4], 1.0)
+        ones = held.tile([SAMPLES, WIDEST], F32, name="ones")
+        nc.gpsimd.memset(ones[:], 1.0)
 
         pair = held.tile([SAMPLES, 16], F32, name="pair")
         nc.vector.tensor_tensor(
@@ -60,12 +55,19 @@ def tile_corrlosschamfer_kernel(tc, verts, cams, offs, out):
             quat.unsqueeze(1).to_broadcast([SAMPLES, 4, 4]),
             ALU.mult,
         )
+        sumsq = held.tile([SAMPLES, 1], F32, name="sumsq")
+        nc.vector.reduce_sum(sumsq[:], pair[:, 0:16:5], axis=mybir.AxisListType.X)
+        norm = held.tile([SAMPLES, 1], F32, name="norm")
+        nc.gpsimd.tensor_tensor(norm[:], sumsq[:], half[:], ALU.pow)
+
+        base = held.tile([SAMPLES, 1], F32, name="base")
+        nc.vector.tensor_scalar(base[:], sumsq[:], 0.5, 0.5 * EPS * EPS, ALU.mult, ALU.add)
 
         def pr(i, j):
             return pair[:, 4 * i + j : 4 * i + j + 1]
 
         mixes = held.tile([SAMPLES, 6], F32, name="mixes")
-        mix = {(r, k): mixes[:, 3 * r + k : 3 * r + k + 1] for r in range(2) for k in range(3)}
+        mix = {(r, k): mixes[:, 2 * k + r : 2 * k + r + 1] for r in range(2) for k in range(3)}
         nc.vector.tensor_scalar(mix[0, 0], pr(QY, QY), pr(QZ, QZ), -1.0, ALU.add, ALU.mult)
         nc.vector.tensor_tensor(mix[0, 1], pr(QX, QY), pr(QW, QZ), ALU.subtract)
         nc.vector.tensor_tensor(mix[0, 2], pr(QX, QZ), pr(QW, QY), ALU.add)
@@ -73,58 +75,47 @@ def tile_corrlosschamfer_kernel(tc, verts, cams, offs, out):
         nc.vector.tensor_scalar(mix[1, 1], pr(QX, QX), pr(QZ, QZ), -1.0, ALU.add, ALU.mult)
         nc.vector.tensor_tensor(mix[1, 2], pr(QY, QZ), pr(QW, QX), ALU.subtract)
 
-        norm_eps = held.tile([SAMPLES, 1], F32, name="norm_eps")
-        nc.vector.tensor_scalar_add(norm_eps[:], norm[:], EPS)
-        inv_norm = held.tile([SAMPLES, 1], F32, name="inv_norm")
-        nc.vector.reciprocal(inv_norm[:], norm_eps[:])
-        gain = held.tile([SAMPLES, 1], F32, name="gain")
-        nc.vector.tensor_scalar(gain[:], inv_norm[:], inv_norm[:, 0:1], 2.0, ALU.mult, ALU.mult)
-        rot = held.tile([SAMPLES, 6], F32, name="rot")
+        half_square = held.tile([SAMPLES, 1], F32, name="half_square")
+        nc.vector.scalar_tensor_tensor(half_square[:], norm[:], EPS, base[:], ALU.mult, ALU.add)
+        numer = held.tile([SAMPLES, 6], F32, name="numer")
         nc.vector.scalar_tensor_tensor(
-            rot[:], mixes[:], gain[:, 0:1], diagonal[:], ALU.mult, ALU.add
+            numer[:], diagonal[:], half_square[:, 0:1], mixes[:], ALU.mult, ALU.add
         )
-        row0, row1 = rot[:, 0:3], rot[:, 3:6]
+        numer_by_k = numer[:].rearrange("p (k r) -> p k r", r=2)
+        gain = held.tile([SAMPLES, 1], F32, name="gain")
+        nc.vector.reciprocal(gain[:], half_square[:])
 
-        rot_sq = held.tile([SAMPLES, 6], F32, name="rot_sq")
-        nc.vector.tensor_tensor(rot_sq[:], rot[:], rot[:], ALU.mult)
-        step = held.tile([SAMPLES, 3], F32, name="step")
-        nc.vector.tensor_tensor(step[:], row0, row1, ALU.subtract)
-        row0_wins = held.tile([SAMPLES, 3], F32, name="row0_wins")
-        nc.vector.tensor_tensor(row0_wins[:], rot_sq[:, 0:3], rot_sq[:, 3:6], ALU.is_ge)
+        larger = held.tile([SAMPLES, 3], F32, name="larger")
+        nc.vector.tensor_reduce(
+            larger[:], numer_by_k, axis=mybir.AxisListType.X, op=ALU.max, apply_absolute_value=True
+        )
 
-        spread = []
-        for k in range(3):
-            spread.append(held.tile([SAMPLES, WIDEST], F32, name=f"spread{k}"))
+        spread = [held.tile([SAMPLES, WIDEST], F32, name=f"spread{k}") for k in range(3)]
+        nc.vector.tensor_scalar(
+            spread[0][:], ones[:], larger[:, 0:1], gain[:, 0:1], ALU.mult, ALU.mult
+        )
+        for k in (1, 2):
             nc.scalar.activation(
                 spread[k][:],
-                step[:, k : k + 1].to_broadcast([SAMPLES, WIDEST]),
+                larger[:, k : k + 1].to_broadcast([SAMPLES, WIDEST]),
                 ACT.Identity,
-                bias=rot[:, 3 + k : 4 + k],
-                scale=row0_wins[:, k : k + 1],
+                scale=gain[:, 0:1],
             )
 
-        pivot_sq = held.tile([SAMPLES, 3], F32, name="pivot_sq")
-        nc.vector.tensor_tensor(pivot_sq[:], rot_sq[:, 0:3], rot_sq[:, 3:6], ALU.max)
-        taken = held.tile([SAMPLES, 3], F32, name="taken")
-        nc.vector.tensor_tensor(taken[:], step[:], row0_wins[:], ALU.mult)
         divisor = held.tile([SAMPLES, 3], F32, name="divisor")
-        nc.vector.tensor_scalar_add(divisor[:], pivot_sq[:], TINY)
-        pivot = held.tile([SAMPLES, 3], F32, name="pivot")
-        nc.vector.tensor_tensor(pivot[:], row1, taken[:], ALU.add)
+        nc.vector.tensor_scalar_max(divisor[:], larger[:], TINY)
         inv_divisor = held.tile([SAMPLES, 3], F32, name="inv_divisor")
         nc.vector.reciprocal(inv_divisor[:], divisor[:])
-        weight = held.tile([SAMPLES, 3], F32, name="weight")
-        nc.vector.scalar_tensor_tensor(
-            weight[:], pivot[:], scale, inv_divisor[:], ALU.mult, ALU.mult
-        )
         factors = held.tile([SAMPLES, 6], F32, name="factors")
-        nc.vector.tensor_tensor(
-            factors[:].rearrange("p (r k) -> p r k", r=2),
-            rot[:].rearrange("p (r k) -> p r k", r=2),
-            weight[:].unsqueeze(1).to_broadcast([SAMPLES, 2, 3]),
+        nc.vector.scalar_tensor_tensor(
+            factors[:].rearrange("p (k r) -> p k r", r=2),
+            numer_by_k,
+            scale,
+            inv_divisor[:].unsqueeze(2).to_broadcast([SAMPLES, 3, 2]),
+            ALU.mult,
             ALU.mult,
         )
-        factor = {(r, k): factors[:, 3 * r + k : 3 * r + k + 1] for r in range(2) for k in range(3)}
+        factor = {(r, k): factors[:, 2 * k + r : 2 * k + r + 1] for r in range(2) for k in range(3)}
 
         weights0 = []
         for k in range(3):
@@ -135,24 +126,24 @@ def tile_corrlosschamfer_kernel(tc, verts, cams, offs, out):
         for width in PIECES:
             piece_offsets = offsets[:, first // 16 : (first + width) // 16]
             total0 = sums.tile([SAMPLES, width], F32, name="total0")
-            total1 = None
+            picked = []
             for k in range(3):
-                picked = work.tile([SAMPLES, width], F32, name=f"picked{k}")
+                picked.append(work.tile([SAMPLES, width], F32, name=f"picked{k}"))
                 nc.vector.tensor_tensor(
-                    picked[:], coords[k][:].indirect(piece_offsets), spread[k][:, 0:width], ALU.mult
+                    picked[k][:], coords[k][:].indirect(piece_offsets), spread[k][:, 0:width], ALU.mult
                 )
                 nc.tensor.matmul(
-                    total0[:], weights0[k][:], picked[:], start=(k == 0), stop=(k == 2)
+                    total0[:], weights0[k][:], picked[k][:], start=(k == 0), stop=(k == 2)
                 )
+            total1 = work.tile([SAMPLES, width], F32, name="total10")
+            nc.scalar.activation(
+                total1[:], picked[0][:], ACT.Identity, bias=shift[1], scale=factor[1, 0]
+            )
+            for k in (1, 2):
                 summed = work.tile([SAMPLES, width], F32, name=f"total1{k}")
-                if k == 0:
-                    nc.scalar.activation(
-                        summed[:], picked[:], ACT.Identity, bias=shift[1], scale=factor[1, 0]
-                    )
-                else:
-                    nc.vector.scalar_tensor_tensor(
-                        summed[:], picked[:], factor[1, k], total1[:], ALU.mult, ALU.add
-                    )
+                nc.vector.scalar_tensor_tensor(
+                    summed[:], picked[k][:], factor[1, k], total1[:], ALU.mult, ALU.add
+                )
                 total1 = summed
             nc.sync.dma_start(out[SAMPLES : 2 * SAMPLES, first : first + width], total1[:])
             image0 = work.tile([SAMPLES, width], F32, name="image0")

@@ -22,7 +22,7 @@ def tile_corrlosschamfer_kernel(tc, verts, cams, offs, out):
     with (
         tc.tile_pool(name="held", bufs=1) as held,
         tc.tile_pool(name="work", bufs=len(PIECES)) as work,
-        tc.psum_pool(name="sums", bufs=2) as sums,
+        tc.psum_pool(name="sums", bufs=len(PIECES)) as sums,
     ):
         offsets = held.tile([128, PICKS // 16], U16, name="offsets")
         nc.sync.dma_start(offsets[:], offs)
@@ -124,6 +124,7 @@ def tile_corrlosschamfer_kernel(tc, verts, cams, offs, out):
 
         first = 0
         for width in PIECES:
+            columns = slice(first, first + width)
             piece_offsets = offsets[:, first // 16 : (first + width) // 16]
             total0 = sums.tile([SAMPLES, width], F32, name="total0")
             picked = []
@@ -135,18 +136,22 @@ def tile_corrlosschamfer_kernel(tc, verts, cams, offs, out):
                 nc.tensor.matmul(
                     total0[:], weights0[k][:], picked[k][:], start=(k == 0), stop=(k == 2)
                 )
-            total1 = work.tile([SAMPLES, width], F32, name="total10")
+            image = work.tile([SAMPLES, 2, width], F32, name="image")
+            one_term = work.tile([SAMPLES, width], F32, name="one_term")
             nc.scalar.activation(
-                total1[:], picked[0][:], ACT.Identity, bias=shift[1], scale=factor[1, 0]
+                one_term[:], picked[0][:], ACT.Identity, bias=shift[1], scale=factor[1, 0]
             )
-            for k in (1, 2):
-                summed = work.tile([SAMPLES, width], F32, name=f"total1{k}")
-                nc.vector.scalar_tensor_tensor(
-                    summed[:], picked[k][:], factor[1, k], total1[:], ALU.mult, ALU.add
-                )
-                total1 = summed
-            nc.sync.dma_start(out[SAMPLES : 2 * SAMPLES, first : first + width], total1[:])
-            image0 = work.tile([SAMPLES, width], F32, name="image0")
-            nc.scalar.activation(image0[:], total0[:], ACT.Identity, bias=shift[0])
-            nc.sync.dma_start(out[0:SAMPLES, first : first + width], image0[:])
+            two_terms = work.tile([SAMPLES, width], F32, name="two_terms")
+            nc.vector.scalar_tensor_tensor(
+                two_terms[:], picked[1][:], factor[1, 1], one_term[:], ALU.mult, ALU.add
+            )
+            nc.vector.scalar_tensor_tensor(
+                image[:, 1, :], picked[2][:], factor[1, 2], two_terms[:], ALU.mult, ALU.add
+            )
+            nc.scalar.activation(image[:, 0, :], total0[:], ACT.Identity, bias=shift[0])
+            if first + width < PICKS:
+                for r in (1, 0):
+                    nc.sync.dma_start(out[r * SAMPLES : (r + 1) * SAMPLES, columns], image[:, r, :])
+            else:
+                nc.sync.dma_start(out.rearrange("(r p) c -> p r c", r=2)[:, :, columns], image[:])
             first += width

@@ -24,15 +24,14 @@ def tile_corrlosschamfer_kernel(tc, verts, cams, offs, out):
         tc.tile_pool(name="work", bufs=len(PIECES)) as work,
         tc.psum_pool(name="sums", bufs=len(PIECES)) as sums,
     ):
+        cam = held.tile([SAMPLES, 7], F32, name="cam")
+        nc.sync.dma_start(cam[:], cams)
         offsets = held.tile([128, PICKS // 16], U16, name="offsets")
         nc.sync.dma_start(offsets[:], offs)
-        cam = held.tile([SAMPLES, 7], F32, name="cam")
-        nc.scalar.dma_start(cam[:], cams)
-        coords = []
-        for k in range(3):
-            coord = held.tile([SAMPLES, VERTICES], F32, name=f"coord{k}")
-            nc.sync.dma_start(coord[:], verts[k * SAMPLES : (k + 1) * SAMPLES, :])
-            coords.append(coord)
+        coords = [held.tile([SAMPLES, VERTICES], F32, name=f"coord{k}") for k in range(3)]
+        nc.scalar.dma_start(coords[0][:], verts[0:SAMPLES, :])
+        for k in (1, 2):
+            nc.sync.dma_start(coords[k][:], verts[k * SAMPLES : (k + 1) * SAMPLES, :])
         scale = cam[:, 0:1]
         shift = [cam[:, 1:2], cam[:, 2:3]]
         quat = cam[:, 3:7]
@@ -45,8 +44,19 @@ def tile_corrlosschamfer_kernel(tc, verts, cams, offs, out):
         nc.gpsimd.memset(diagonal[:], 0.0)
         nc.gpsimd.memset(diagonal[:, 0:1], 1.0)
         nc.gpsimd.memset(diagonal[:, 3:4], 1.0)
+        diagonal_eps = held.tile([SAMPLES, 6], F32, name="diagonal_eps")
+        nc.gpsimd.memset(diagonal_eps[:], 0.0)
+        nc.gpsimd.memset(diagonal_eps[:, 0:1], EPS)
+        nc.gpsimd.memset(diagonal_eps[:, 3:4], EPS)
+        rootless_tile = held.tile([SAMPLES, 9], F32, name="rootless_tile")
+        nc.gpsimd.memset(rootless_tile[:], TINY)
+        rootless_and_floor = rootless_tile[:].rearrange("p (k c) -> p k c", c=3)
+        rootless = rootless_and_floor[:, :, 0:2]
         ones = held.tile([SAMPLES, WIDEST], F32, name="ones")
         nc.gpsimd.memset(ones[:], 1.0)
+
+        def by_k(six):
+            return six[:].rearrange("p (k r) -> p k r", r=2)
 
         pair = held.tile([SAMPLES, 16], F32, name="pair")
         nc.vector.tensor_tensor(
@@ -75,43 +85,48 @@ def tile_corrlosschamfer_kernel(tc, verts, cams, offs, out):
         nc.vector.tensor_scalar(mix[1, 1], pr(QX, QX), pr(QZ, QZ), -1.0, ALU.add, ALU.mult)
         nc.vector.tensor_tensor(mix[1, 2], pr(QY, QZ), pr(QW, QX), ALU.subtract)
 
-        half_square = held.tile([SAMPLES, 1], F32, name="half_square")
-        nc.vector.scalar_tensor_tensor(half_square[:], norm[:], EPS, base[:], ALU.mult, ALU.add)
-        numer = held.tile([SAMPLES, 6], F32, name="numer")
         nc.vector.scalar_tensor_tensor(
-            numer[:], diagonal[:], half_square[:, 0:1], mixes[:], ALU.mult, ALU.add
+            rootless, by_k(diagonal), base[:, 0:1], by_k(mixes), ALU.mult, ALU.add
         )
-        numer_by_k = numer[:].rearrange("p (k r) -> p k r", r=2)
-        gain = held.tile([SAMPLES, 1], F32, name="gain")
-        nc.vector.reciprocal(gain[:], half_square[:])
-
         larger = held.tile([SAMPLES, 3], F32, name="larger")
         nc.vector.tensor_reduce(
-            larger[:], numer_by_k, axis=mybir.AxisListType.X, op=ALU.max, apply_absolute_value=True
+            larger[:], rootless_and_floor, axis=mybir.AxisListType.X, op=ALU.max, apply_absolute_value=True
         )
+        inv_base = held.tile([SAMPLES, 1], F32, name="inv_base")
+        nc.vector.reciprocal(inv_base[:], base[:])
 
         spread = [held.tile([SAMPLES, WIDEST], F32, name=f"spread{k}") for k in range(3)]
         nc.vector.tensor_scalar(
-            spread[0][:], ones[:], larger[:, 0:1], gain[:, 0:1], ALU.mult, ALU.mult
+            spread[0][:], ones[:], larger[:, 0:1], inv_base[:, 0:1], ALU.mult, ALU.mult
         )
         for k in (1, 2):
             nc.scalar.activation(
                 spread[k][:],
                 larger[:, k : k + 1].to_broadcast([SAMPLES, WIDEST]),
                 ACT.Identity,
-                scale=gain[:, 0:1],
+                scale=inv_base[:, 0:1],
             )
 
-        divisor = held.tile([SAMPLES, 3], F32, name="divisor")
-        nc.vector.tensor_scalar_max(divisor[:], larger[:], TINY)
-        inv_divisor = held.tile([SAMPLES, 3], F32, name="inv_divisor")
-        nc.vector.reciprocal(inv_divisor[:], divisor[:])
+        inv_larger = held.tile([SAMPLES, 3], F32, name="inv_larger")
+        nc.vector.reciprocal(inv_larger[:], larger[:])
+        scale_by_pivot = held.tile([SAMPLES, 3], F32, name="scale_by_pivot")
+        nc.vector.tensor_scalar(
+            scale_by_pivot[:], inv_larger[:], scale, base[:, 0:1], ALU.mult, ALU.mult
+        )
+        numer = held.tile([SAMPLES, 6], F32, name="numer")
+        nc.vector.scalar_tensor_tensor(
+            by_k(numer), by_k(diagonal_eps), norm[:, 0:1], rootless, ALU.mult, ALU.add
+        )
+        halved = held.tile([SAMPLES, 1], F32, name="halved")
+        nc.vector.scalar_tensor_tensor(halved[:], norm[:], EPS, base[:], ALU.mult, ALU.add)
+        inv_halved = held.tile([SAMPLES, 1], F32, name="inv_halved")
+        nc.vector.reciprocal(inv_halved[:], halved[:])
         factors = held.tile([SAMPLES, 6], F32, name="factors")
         nc.vector.scalar_tensor_tensor(
-            factors[:].rearrange("p (k r) -> p k r", r=2),
-            numer_by_k,
-            scale,
-            inv_divisor[:].unsqueeze(2).to_broadcast([SAMPLES, 3, 2]),
+            by_k(factors),
+            by_k(numer),
+            inv_halved[:, 0:1],
+            scale_by_pivot[:].unsqueeze(2).to_broadcast([SAMPLES, 3, 2]),
             ALU.mult,
             ALU.mult,
         )

@@ -25,12 +25,11 @@ def tile_corrlosschamfer_kernel(tc, verts, cams, offs, out):
         tc.psum_pool(name="sums", bufs=len(PIECES)) as sums,
     ):
         cam = held.tile([SAMPLES, 7], F32, name="cam")
-        nc.sync.dma_start(cam[:], cams)
+        nc.scalar.dma_start(cam[:], cams)
         offsets = held.tile([128, PICKS // 16], U16, name="offsets")
         nc.sync.dma_start(offsets[:], offs)
         coords = [held.tile([SAMPLES, VERTICES], F32, name=f"coord{k}") for k in range(3)]
-        nc.scalar.dma_start(coords[0][:], verts[0:SAMPLES, :])
-        for k in (1, 2):
+        for k in range(3):
             nc.sync.dma_start(coords[k][:], verts[k * SAMPLES : (k + 1) * SAMPLES, :])
         scale = cam[:, 0:1]
         shift = [cam[:, 1:2], cam[:, 2:3]]

@@ -25,11 +25,12 @@ def tile_corrlosschamfer_kernel(tc, verts, cams, offs, out):
         tc.psum_pool(name="sums", bufs=len(PIECES)) as sums,
     ):
         cam = held.tile([SAMPLES, 7], F32, name="cam")
-        nc.scalar.dma_start(cam[:], cams)
+        nc.sync.dma_start(cam[:], cams)
+        coords = [held.tile([SAMPLES, VERTICES], F32, name=f"coord{k}") for k in range(3)]
+        nc.sync.dma_start(coords[0][:], verts[0:SAMPLES, :])
         offsets = held.tile([128, PICKS // 16], U16, name="offsets")
         nc.sync.dma_start(offsets[:], offs)
-        coords = [held.tile([SAMPLES, VERTICES], F32, name=f"coord{k}") for k in range(3)]
-        for k in range(3):
+        for k in (1, 2):
             nc.sync.dma_start(coords[k][:], verts[k * SAMPLES : (k + 1) * SAMPLES, :])
         scale = cam[:, 0:1]
         shift = [cam[:, 1:2], cam[:, 2:3]]

import concourse.mybir as mybir
from concourse.masks import make_identity

F32 = mybir.dt.float32
U16 = mybir.dt.uint16
ALU = mybir.AluOpType
ACT = mybir.ActivationFunctionType

SAMPLES = 128
VERTICES = 2048
PICKS = 2048
PIECES = (512, 512, 512, 384, 128)
WIDEST = max(PIECES)
assert sum(PIECES) == PICKS and all(width % 32 == 0 for width in PIECES)
EPS = 1e-8
TINY = 1e-30
QW, QX, QY, QZ = 0, 1, 2, 3


def tile_corrlosschamfer_kernel(tc, verts, cams, offs, out):
    nc = tc.nc
    with (
        tc.tile_pool(name="held", bufs=1) as held,
        tc.tile_pool(name="work", bufs=len(PIECES)) as work,
        tc.psum_pool(name="sums", bufs=len(PIECES)) as sums,
    ):
        cam = held.tile([SAMPLES, 7], F32, name="cam")
        nc.sync.dma_start(cam[:], cams)
        coords = [held.tile([SAMPLES, VERTICES], F32, name=f"coord{k}") for k in range(3)]
        nc.sync.dma_start(coords[0][:], verts[0:SAMPLES, :])
        offsets = held.tile([128, PICKS // 16], U16, name="offsets")
        nc.sync.dma_start(offsets[:], offs)
        for k in (1, 2):
            nc.sync.dma_start(coords[k][:], verts[k * SAMPLES : (k + 1) * SAMPLES, :])
        scale = cam[:, 0:1]
        shift = [cam[:, 1:2], cam[:, 2:3]]
        quat = cam[:, 3:7]

        identity = held.tile([SAMPLES, SAMPLES], F32, name="identity")
        make_identity(nc, identity[:])
        half = held.tile([SAMPLES, 1], F32, name="half")
        nc.gpsimd.memset(half[:], 0.5)
        diagonal = held.tile([SAMPLES, 6], F32, name="diagonal")
        nc.gpsimd.memset(diagonal[:], 0.0)
        nc.gpsimd.memset(diagonal[:, 0:1], 1.0)
        nc.gpsimd.memset(diagonal[:, 3:4], 1.0)
        diagonal_eps = held.tile([SAMPLES, 6], F32, name="diagonal_eps")
        nc.gpsimd.memset(diagonal_eps[:], 0.0)
        nc.gpsimd.memset(diagonal_eps[:, 0:1], EPS)
        nc.gpsimd.memset(diagonal_eps[:, 3:4], EPS)
        rootless_tile = held.tile([SAMPLES, 9], F32, name="rootless_tile")
        nc.gpsimd.memset(rootless_tile[:], TINY)
        rootless_and_floor = rootless_tile[:].rearrange("p (k c) -> p k c", c=3)
        rootless = rootless_and_floor[:, :, 0:2]
        ones = held.tile([SAMPLES, WIDEST], F32, name="ones")
        nc.gpsimd.memset(ones[:], 1.0)

        def by_k(six):
            return six[:].rearrange("p (k r) -> p k r", r=2)

        pair = held.tile([SAMPLES, 16], F32, name="pair")
        nc.vector.tensor_tensor(
            pair[:].rearrange("p (i j) -> p i j", i=4),
            quat.unsqueeze(2).to_broadcast([SAMPLES, 4, 4]),
            quat.unsqueeze(1).to_broadcast([SAMPLES, 4, 4]),
            ALU.mult,
        )
        sumsq = held.tile([SAMPLES, 1], F32, name="sumsq")
        nc.vector.reduce_sum(sumsq[:], pair[:, 0:16:5], axis=mybir.AxisListType.X)
        norm = held.tile([SAMPLES, 1], F32, name="norm")
        nc.gpsimd.tensor_tensor(norm[:], sumsq[:], half[:], ALU.pow)

        base = held.tile([SAMPLES, 1], F32, name="base")
        nc.vector.tensor_scalar(base[:], sumsq[:], 0.5, 0.5 * EPS * EPS, ALU.mult, ALU.add)

        def pr(i, j):
            return pair[:, 4 * i + j : 4 * i + j + 1]

        mixes = held.tile([SAMPLES, 6], F32, name="mixes")
        mix = {(r, k): mixes[:, 2 * k + r : 2 * k + r + 1] for r in range(2) for k in range(3)}
        nc.vector.tensor_scalar(mix[0, 0], pr(QY, QY), pr(QZ, QZ), -1.0, ALU.add, ALU.mult)
        nc.vector.tensor_tensor(mix[0, 1], pr(QX, QY), pr(QW, QZ), ALU.subtract)
        nc.vector.tensor_tensor(mix[0, 2], pr(QX, QZ), pr(QW, QY), ALU.add)
        nc.vector.tensor_tensor(mix[1, 0], pr(QX, QY), pr(QW, QZ), ALU.add)
        nc.vector.tensor_scalar(mix[1, 1], pr(QX, QX), pr(QZ, QZ), -1.0, ALU.add, ALU.mult)
        nc.vector.tensor_tensor(mix[1, 2], pr(QY, QZ), pr(QW, QX), ALU.subtract)

        nc.vector.scalar_tensor_tensor(
            rootless, by_k(diagonal), base[:, 0:1], by_k(mixes), ALU.mult, ALU.add
        )
        larger = held.tile([SAMPLES, 3], F32, name="larger")
        nc.vector.tensor_reduce(
            larger[:], rootless_and_floor, axis=mybir.AxisListType.X, op=ALU.max, apply_absolute_value=True
        )
        inv_base = held.tile([SAMPLES, 1], F32, name="inv_base")
        nc.vector.reciprocal(inv_base[:], base[:])

        spread = [held.tile([SAMPLES, WIDEST], F32, name=f"spread{k}") for k in range(3)]
        nc.vector.tensor_scalar(
            spread[0][:], ones[:], larger[:, 0:1], inv_base[:, 0:1], ALU.mult, ALU.mult
        )
        for k in (1, 2):
            nc.scalar.activation(
                spread[k][:],
                larger[:, k : k + 1].to_broadcast([SAMPLES, WIDEST]),
                ACT.Identity,
                scale=inv_base[:, 0:1],
            )

        inv_larger = held.tile([SAMPLES, 3], F32, name="inv_larger")
        nc.vector.reciprocal(inv_larger[:], larger[:])
        scale_by_pivot = held.tile([SAMPLES, 3], F32, name="scale_by_pivot")
        nc.vector.tensor_scalar(
            scale_by_pivot[:], inv_larger[:], scale, base[:, 0:1], ALU.mult, ALU.mult
        )
        numer = held.tile([SAMPLES, 6], F32, name="numer")
        nc.vector.scalar_tensor_tensor(
            by_k(numer), by_k(diagonal_eps), norm[:, 0:1], rootless, ALU.mult, ALU.add
        )
        halved = held.tile([SAMPLES, 1], F32, name="halved")
        nc.vector.scalar_tensor_tensor(halved[:], norm[:], EPS, base[:], ALU.mult, ALU.add)
        inv_halved = held.tile([SAMPLES, 1], F32, name="inv_halved")
        nc.vector.reciprocal(inv_halved[:], halved[:])
        factors = held.tile([SAMPLES, 6], F32, name="factors")
        nc.vector.scalar_tensor_tensor(
            by_k(factors),
            by_k(numer),
            inv_halved[:, 0:1],
            scale_by_pivot[:].unsqueeze(2).to_broadcast([SAMPLES, 3, 2]),
            ALU.mult,
            ALU.mult,
        )
        factor = {(r, k): factors[:, 2 * k + r : 2 * k + r + 1] for r in range(2) for k in range(3)}

        weights0 = []
        for k in range(3):
            weights0.append(held.tile([SAMPLES, SAMPLES], F32, name=f"weights0{k}"))
            nc.scalar.activation(weights0[k][:], identity[:], ACT.Identity, scale=factor[0, k])

        first = 0
        for width in PIECES:
            columns = slice(first, first + width)
            piece_offsets = offsets[:, first // 16 : (first + width) // 16]
            total0 = sums.tile([SAMPLES, width], F32, name="total0")
            picked = []
            for k in range(3):
                picked.append(work.tile([SAMPLES, width], F32, name=f"picked{k}"))
                nc.vector.tensor_tensor(
                    picked[k][:], coords[k][:].indirect(piece_offsets), spread[k][:, 0:width], ALU.mult
                )
                nc.tensor.matmul(
                    total0[:], weights0[k][:], picked[k][:], start=(k == 0), stop=(k == 2)
                )
            image = work.tile([SAMPLES, 2, width], F32, name="image")
            one_term = work.tile([SAMPLES, width], F32, name="one_term")
            nc.scalar.activation(
                one_term[:], picked[0][:], ACT.Identity, bias=shift[1], scale=factor[1, 0]
            )
            two_terms = work.tile([SAMPLES, width], F32, name="two_terms")
            nc.vector.scalar_tensor_tensor(
                two_terms[:], picked[1][:], factor[1, 1], one_term[:], ALU.mult, ALU.add
            )
            nc.vector.scalar_tensor_tensor(
                image[:, 1, :], picked[2][:], factor[1, 2], two_terms[:], ALU.mult, ALU.add
            )
            nc.scalar.activation(image[:, 0, :], total0[:], ACT.Identity, bias=shift[0])
            if first + width < PICKS:
                for r in (1, 0):
                    nc.sync.dma_start(out[r * SAMPLES : (r + 1) * SAMPLES, columns], image[:, r, :])
            else:
                nc.sync.dma_start(out.rearrange("(r p) c -> p r c", r=2)[:, :, columns], image[:])
            first += width
